import numpy as np
import ml_dtypes


def mxq(x, axis, fmt="e4m3"):
    dtype, down = {"e4m3": (ml_dtypes.float8_e4m3fn, 7), "e5m2": (ml_dtypes.float8_e5m2, 14)}[fmt]
    v = np.moveaxis(np.asarray(x, np.float32).astype(ml_dtypes.bfloat16).astype(np.float64), axis, -1)
    blocks = v.reshape(v.shape[:-1] + (-1, 32))
    amax = np.abs(blocks).max(-1, keepdims=True)
    byte = np.maximum(np.where(amax > 0, np.frexp(amax)[1] - 1 + 127, 0) - down, 1)
    scale = np.exp2(byte - 127.0)
    codes = (blocks / scale).astype(np.float32).astype(dtype).astype(np.float64)
    return np.moveaxis((codes * scale).reshape(v.shape), -1, axis)


WIDE = False


def mx_kscale(k):
    if not WIDE:
        return np.ones(k)
    levels = np.array([10, -10, 5, -5, 0])
    a = np.random.permutation(np.resize(levels, k // 512 * 4)).reshape(k // 512, 4)
    idx = np.arange(k)
    return np.exp2(a[idx // 512, idx % 128 // 32])


BF16 = ml_dtypes.bfloat16


def bf(x):
    return np.asarray(x, np.float32).astype(BF16)


def f64(x):
    return np.asarray(x).astype(np.float64)


B, S, HID, H, D = 4, 2048, 512, 2, 64
QKV = 3 * H * D


def rotate_half(x):
    x1, x2 = x[..., : x.shape[-1] // 2], x[..., x.shape[-1] // 2 :]
    return np.concatenate((-x2, x1), axis=-1)


def setup_inputs():
    s = mx_kscale(HID)
    return {"hidden_states": bf(np.random.standard_normal((B, S, HID)) * s),
            "cos": bf(np.random.uniform(size=(S, D))),
            "sin": bf(np.random.uniform(size=(S, D))),
            "w_qkv": bf(np.random.standard_normal((HID, QKV)) * 2.0 / np.sqrt(HID) / s[:, None])}


def reference(hidden_states, cos, sin, w_qkv):
    qkv = mxq(f64(hidden_states), 2, "e4m3") @ mxq(f64(w_qkv), 0, "e4m3")
    qkv = qkv.reshape(B, S, 3 * H, D)
    q, k, v = qkv[:, :, :H], qkv[:, :, H:2 * H], qkv[:, :, 2 * H:]
    c = f64(cos)[:, None, :]
    sn = f64(sin)[:, None, :]
    q_rot = q * c + rotate_half(q) * sn
    k_rot = k * c + rotate_half(k) * sn
    return q_rot, k_rot, v

@@ -1,0 +1,259 @@
+from contextlib import ExitStack
+
+import concourse.mybir as mybir
+from concourse.masks import make_identity
+
+F32 = mybir.dt.float32
+BF16 = mybir.dt.bfloat16
+U32 = mybir.dt.uint32
+U8 = mybir.dt.uint8
+FP8X4 = mybir.dt.float8_e4m3fn_x4
+MULT = mybir.AluOpType.mult
+ADD = mybir.AluOpType.add
+
+P = 128
+BATCH = 4
+SEQ = 2048
+HID = 512
+HEAD = 64
+HALF = 32
+QK_COLS = 256
+V_COLS = 128
+T_PER_PART = SEQ // P
+TILES = 4
+GROUPS_PER_BATCH = T_PER_PART // TILES
+N_GROUPS = BATCH * GROUPS_PER_BATCH
+
+FLOPS = 2 * BATCH * SEQ * HID * (QK_COLS + V_COLS)
+
+
+def tile_attention_pa_t_kernel(tc, hidden_states, cos, sin, w_qkv, out_0, out_1, out_2):
+    nc = tc.nc
+    xv = hidden_states.rearrange("b (p t) k -> b p t k", t=T_PER_PART)
+    qv = out_0.rearrange("b (p t) h d -> b p t (h d)", t=T_PER_PART)
+    kv = out_1.rearrange("b (p t) h d -> b p t (h d)", t=T_PER_PART)
+    vv = out_2.rearrange("b (p t) h d -> b p t (h d)", t=T_PER_PART)
+
+    with ExitStack() as ctx:
+        const = ctx.enter_context(tc.tile_pool(name="const", bufs=1))
+        xpool = ctx.enter_context(tc.tile_pool(name="xpool", bufs=N_GROUPS))
+        gpool = ctx.enter_context(tc.tile_pool(name="gpool", bufs=3))
+        cpool = ctx.enter_context(tc.tile_pool(name="cpool", bufs=3))
+        rpool = ctx.enter_context(tc.tile_pool(name="rpool", bufs=3))
+        opool = ctx.enter_context(tc.tile_pool(name="opool", bufs=N_GROUPS))
+        ps_x = ctx.enter_context(tc.psum_pool(name="ps_x", bufs=2))
+        ps_qk = ctx.enter_context(tc.psum_pool(name="ps_qk", bufs=4))
+        ps_v = ctx.enter_context(tc.psum_pool(name="ps_v", bufs=2))
+        ctx.enter_context(tc.manual_schedule())
+
+        x_tiles = {}
+        xt_tiles = {}
+        grouped_tiles = {}
+        code_tiles = {}
+        qk_banks = {}
+        v_banks = {}
+        prod_tiles = {}
+        out_tiles = {}
+
+        ident = const.tile([P, P], F32, name="ident")
+        make_identity(nc, ident[:])
+
+        w_raw = const.tile([P, 4 * (QK_COLS + V_COLS)], BF16, name="w_raw")
+        w_grp = const.tile([P, 4 * (QK_COLS + V_COLS)], BF16, name="w_grp", align_bytes=64)
+        w_codes = const.tile([P, QK_COLS + V_COLS], U32, name="w_codes", align_bytes=64)
+        w_scales = const.tile([P, QK_COLS + V_COLS], U8, name="w_scales", align_bytes=64)
+        cos_sb = const.tile([P, T_PER_PART * HEAD], BF16, name="cos_sb")
+        sin_sb = const.tile([P, T_PER_PART * HEAD], BF16, name="sin_sb")
+        cos_v = cos_sb[:].rearrange("p (t d) -> p t d", d=HEAD)
+        sin_v = sin_sb[:].rearrange("p (t d) -> p t d", d=HEAD)
+
+        def load_x(i):
+            b, gg = divmod(i, GROUPS_PER_BATCH)
+            x_sb = xpool.tile([P, TILES * HID], BF16, name="x_sb", tag="x_sb")
+            nc.sync.dma_start(
+                out=x_sb[:].rearrange("p (t k) -> p t k", k=HID),
+                in_=xv[b, :, gg * TILES : (gg + 1) * TILES, :],
+            )
+            x_tiles[i] = x_sb
+
+        def transpose_group(i):
+            words = x_tiles[i][:].bitcast(F32)
+            banks = []
+            for pr in range(2):
+                xt = ps_x.tile([P, 512], F32, name="xt", tag="xt")
+                for j in range(2):
+                    for u in range(2):
+                        col = (2 * pr + j) * 256 + u * P
+                        nc.tensor.transpose(
+                            xt[:, u * 256 + j * P : u * 256 + (j + 1) * P],
+                            words[:, col : col + P],
+                            ident[:],
+                        )
+                banks.append(xt)
+            xt_tiles[i] = banks
+
+        def copy_group(i):
+            grouped = gpool.tile([P, TILES * HID], BF16, name="grouped", tag="grouped", align_bytes=64)
+            gw = grouped[:].bitcast(F32)
+            for pr in range(2):
+                nc.scalar.copy(
+                    out=gw[:, pr * 512 : (pr + 1) * 512].rearrange("p (m u) -> p m u", u=2),
+                    in_=xt_tiles[i][pr][:].rearrange("p (u m) -> p m u", u=2),
+                )
+            grouped_tiles[i] = grouped
+
+        def quantise_group(i):
+            codes = cpool.tile([P, TILES * P], U32, name="codes", tag="codes", align_bytes=64)
+            scales = cpool.tile([P, TILES * P], U8, name="scales", tag="scales", align_bytes=64)
+            nc.vector.quantize_mx(
+                out=codes[:].bitcast(FP8X4), scales=scales[:], in_=grouped_tiles[i][:]
+            )
+            code_tiles[i] = (codes, scales)
+
+        def project_group(i):
+            codes, scales = code_tiles[i]
+            v_ps = ps_v.tile([P, 512], F32, name="v_ps", tag="v_ps")
+            banks = []
+            for pr in range(2):
+                qk_ps = ps_qk.tile([P, 512], F32, name="qk_ps", tag="qk_ps")
+                for j in range(2):
+                    tl = 2 * pr + j
+                    cols = slice(tl * P, (tl + 1) * P)
+                    nc.tensor.matmul_mx(
+                        out=qk_ps[:, j * QK_COLS : (j + 1) * QK_COLS],
+                        lhsT=codes[:, cols].bitcast(FP8X4),
+                        lhsT_scale=scales[:, cols],
+                        rhs=w_codes[:, 0:QK_COLS].bitcast(FP8X4),
+                        rhs_scale=w_scales[:, 0:QK_COLS],
+                        start=True,
+                        stop=True,
+                    )
+                    nc.tensor.matmul_mx(
+                        out=v_ps[:, cols],
+                        lhsT=codes[:, cols].bitcast(FP8X4),
+                        lhsT_scale=scales[:, cols],
+                        rhs=w_codes[:, QK_COLS : QK_COLS + V_COLS].bitcast(FP8X4),
+                        rhs_scale=w_scales[:, QK_COLS : QK_COLS + V_COLS],
+                        start=True,
+                        stop=True,
+                    )
+                banks.append(qk_ps)
+            qk_banks[i] = banks
+            v_banks[i] = v_ps
+
+        def rope_products(i, pr):
+            gg = i % GROUPS_PER_BATCH
+            if pr == 0:
+                pa = rpool.tile([P, TILES * QK_COLS], F32, name="pa", tag="pa")
+                pb = rpool.tile([P, TILES * QK_COLS], F32, name="pb", tag="pb")
+                prod_tiles[i] = (pa, pb)
+            pa, pb = prod_tiles[i]
+            t0 = gg * TILES + 2 * pr
+            bank = qk_banks[i][pr][:].rearrange("p (j h d) -> p j h d", j=2, d=HEAD)
+            pa_v = pa[:].rearrange("p (t h d) -> p t h d", t=TILES, d=HEAD)[:, 2 * pr : 2 * pr + 2, :, :]
+            pb_v = pb[:].rearrange("p (t h d) -> p t h d", t=TILES, d=HEAD)[:, 2 * pr : 2 * pr + 2, :, :]
+            nc.vector.tensor_tensor(
+                out=pa_v,
+                in0=bank,
+                in1=cos_v[:, t0 : t0 + 2, :].unsqueeze(2).to_broadcast([P, 2, 4, HEAD]),
+                op=MULT,
+            )
+            nc.vector.tensor_tensor(
+                out=pb_v[:, :, :, 0:HALF],
+                in0=bank[:, :, :, HALF:HEAD],
+                in1=sin_v[:, t0 : t0 + 2, 0:HALF].unsqueeze(2).to_broadcast([P, 2, 4, HALF]),
+                op=MULT,
+            )
+            nc.vector.tensor_tensor(
+                out=pb_v[:, :, :, HALF:HEAD],
+                in0=bank[:, :, :, 0:HALF],
+                in1=sin_v[:, t0 : t0 + 2, HALF:HEAD].unsqueeze(2).to_broadcast([P, 2, 4, HALF]),
+                op=MULT,
+            )
+
+        def rope_sum(i, engine, t_lo, t_hi):
+            pa, pb = prod_tiles[i]
+            if i not in out_tiles:
+                qk_out = opool.tile([P, 2 * TILES * P], F32, name="qk_out", tag="qk_out")
+                out_tiles[i] = qk_out
+            qk_out = out_tiles[i]
+            engine.tensor_tensor(
+                out=qk_out[:].rearrange("p (g t c) -> p t g c", g=2, c=P)[:, t_lo:t_hi, :, :],
+                in0=pa[:].rearrange("p (t g c) -> p t g c", g=2, c=P)[:, t_lo:t_hi, :, :],
+                in1=pb[:].rearrange("p (t g c) -> p t g c", g=2, c=P)[:, t_lo:t_hi, :, :],
+                op=ADD,
+            )
+
+        def copy_v(i):
+            v_out = opool.tile([P, TILES * P], F32, name="v_out", tag="v_out")
+            nc.scalar.copy(out=v_out[:], in_=v_banks[i][:])
+            return v_out
+
+        def store_group(i, v_out):
+            b, gg = divmod(i, GROUPS_PER_BATCH)
+            ts = slice(gg * TILES, (gg + 1) * TILES)
+            qk_out = out_tiles[i]
+            nc.sync.dma_start(out=vv[b, :, ts, :], in_=v_out[:].rearrange("p (t c) -> p t c", c=P))
+            nc.sync.dma_start(
+                out=qv[b, :, ts, :], in_=qk_out[:, 0 : TILES * P].rearrange("p (t c) -> p t c", c=P)
+            )
+            nc.sync.dma_start(
+                out=kv[b, :, ts, :],
+                in_=qk_out[:, TILES * P : 2 * TILES * P].rearrange("p (t c) -> p t c", c=P),
+            )
+
+        load_x(0)
+        nc.sync.dma_start(
+            out=w_raw[:].rearrange("q (u f) -> q u f", u=2),
+            in_=w_qkv.rearrange("(u q e) c -> q u (e c)", u=2, e=2),
+        )
+        load_x(1)
+        nc.sync.dma_start(out=cos_v, in_=cos.rearrange("(p t) d -> p t d", t=T_PER_PART))
+        nc.sync.dma_start(out=sin_v, in_=sin.rearrange("(p t) d -> p t d", t=T_PER_PART))
+        for i in range(2, N_GROUPS):
+            load_x(i)
+
+        nc.vector.tensor_copy(
+            out=w_grp[:].rearrange("p (c t) -> p c t", t=4),
+            in_=w_raw[:].rearrange("p (t c) -> p c t", t=4),
+        )
+        nc.vector.quantize_mx(
+            out=w_codes[:, 0:QK_COLS].bitcast(FP8X4),
+            scales=w_scales[:, 0:QK_COLS],
+            in_=w_grp[:, 0 : 4 * QK_COLS],
+        )
+        nc.vector.quantize_mx(
+            out=w_codes[:, QK_COLS : QK_COLS + V_COLS].bitcast(FP8X4),
+            scales=w_scales[:, QK_COLS : QK_COLS + V_COLS],
+            in_=w_grp[:, 4 * QK_COLS : 4 * (QK_COLS + V_COLS)],
+        )
+
+        transpose_group(0)
+        copy_group(0)
+        quantise_group(0)
+        transpose_group(1)
+        copy_group(1)
+        quantise_group(1)
+        nc.vector.tensor_scalar_mul(out=sin_v[:, :, 0:HALF], in0=sin_v[:, :, 0:HALF], scalar1=-1.0)
+        project_group(0)
+
+        for i in range(N_GROUPS):
+            if i + 2 < N_GROUPS:
+                transpose_group(i + 2)
+            v_out = copy_v(i)
+            if i + 2 < N_GROUPS:
+                copy_group(i + 2)
+            if i + 1 < N_GROUPS:
+                project_group(i + 1)
+            if i + 1 < N_GROUPS:
+                rope_products(i, 0)
+                rope_products(i, 1)
+                if i + 2 < N_GROUPS:
+                    quantise_group(i + 2)
+                rope_sum(i, nc.gpsimd, 0, TILES)
+            else:
+                rope_products(i, 0)
+                rope_sum(i, nc.gpsimd, 0, 2)
+                rope_products(i, 1)
+                rope_sum(i, nc.vector, 2, TILES)
+            store_group(i, v_out)

@@ -67,79 +67,80 @@ def tile_attention_pa_t_kernel(tc, hidden_states, cos, sin, w_qkv, out_0, out_1,
         cos_v = cos_sb[:].rearrange("p (t d) -> p t d", d=HEAD)
         sin_v = sin_sb[:].rearrange("p (t d) -> p t d", d=HEAD)
 
-        def load_x(i):
+        def load_x(i, t_lo, t_hi):
             b, gg = divmod(i, GROUPS_PER_BATCH)
-            x_sb = xpool.tile([P, TILES * HID], BF16, name="x_sb", tag="x_sb")
+            if i not in x_tiles:
+                x_sb = xpool.tile([P, TILES * HID], BF16, name="x_sb", tag="x_sb")
+                x_tiles[i] = x_sb
             nc.sync.dma_start(
-                out=x_sb[:].rearrange("p (t k) -> p t k", k=HID),
-                in_=xv[b, :, gg * TILES : (gg + 1) * TILES, :],
+                out=x_tiles[i][:, t_lo * HID : t_hi * HID].rearrange("p (t k) -> p t k", k=HID),
+                in_=xv[b, :, gg * TILES + t_lo : gg * TILES + t_hi, :],
             )
-            x_tiles[i] = x_sb
 
-        def transpose_group(i):
+        def transpose_pair(i, pr):
             words = x_tiles[i][:].bitcast(F32)
-            banks = []
-            for pr in range(2):
-                xt = ps_x.tile([P, 512], F32, name="xt", tag="xt")
-                for j in range(2):
-                    for u in range(2):
-                        col = (2 * pr + j) * 256 + u * P
-                        nc.tensor.transpose(
-                            xt[:, u * 256 + j * P : u * 256 + (j + 1) * P],
-                            words[:, col : col + P],
-                            ident[:],
-                        )
-                banks.append(xt)
-            xt_tiles[i] = banks
+            xt = ps_x.tile([P, 512], F32, name="xt", tag="xt")
+            for j in range(2):
+                for u in range(2):
+                    col = (2 * pr + j) * 256 + u * P
+                    nc.tensor.transpose(
+                        xt[:, u * 256 + j * P : u * 256 + (j + 1) * P],
+                        words[:, col : col + P],
+                        ident[:],
+                    )
+            xt_tiles[i, pr] = xt
 
-        def copy_group(i):
-            grouped = gpool.tile([P, TILES * HID], BF16, name="grouped", tag="grouped", align_bytes=64)
-            gw = grouped[:].bitcast(F32)
-            for pr in range(2):
-                nc.scalar.copy(
-                    out=gw[:, pr * 512 : (pr + 1) * 512].rearrange("p (m u) -> p m u", u=2),
-                    in_=xt_tiles[i][pr][:].rearrange("p (u m) -> p m u", u=2),
-                )
-            grouped_tiles[i] = grouped
-
-        def quantise_group(i):
-            codes = cpool.tile([P, TILES * P], U32, name="codes", tag="codes", align_bytes=64)
-            scales = cpool.tile([P, TILES * P], U8, name="scales", tag="scales", align_bytes=64)
-            nc.vector.quantize_mx(
-                out=codes[:].bitcast(FP8X4), scales=scales[:], in_=grouped_tiles[i][:]
+        def copy_pair(i, pr):
+            if pr == 0:
+                grouped = gpool.tile([P, TILES * HID], BF16, name="grouped", tag="grouped", align_bytes=64)
+                grouped_tiles[i] = grouped
+            gw = grouped_tiles[i][:].bitcast(F32)
+            nc.scalar.copy(
+                out=gw[:, pr * 512 : (pr + 1) * 512].rearrange("p (m u) -> p m u", u=2),
+                in_=xt_tiles[i, pr][:].rearrange("p (u m) -> p m u", u=2),
             )
-            code_tiles[i] = (codes, scales)
 
-        def project_group(i):
+        def quantise(i, pr_lo, pr_hi):
+            if pr_lo == 0:
+                codes = cpool.tile([P, TILES * P], U32, name="codes", tag="codes", align_bytes=64)
+                scales = cpool.tile([P, TILES * P], U8, name="scales", tag="scales", align_bytes=64)
+                code_tiles[i] = (codes, scales)
             codes, scales = code_tiles[i]
-            v_ps = ps_v.tile([P, 512], F32, name="v_ps", tag="v_ps")
-            banks = []
-            for pr in range(2):
-                qk_ps = ps_qk.tile([P, 512], F32, name="qk_ps", tag="qk_ps")
-                for j in range(2):
-                    tl = 2 * pr + j
-                    cols = slice(tl * P, (tl + 1) * P)
-                    nc.tensor.matmul_mx(
-                        out=qk_ps[:, j * QK_COLS : (j + 1) * QK_COLS],
-                        lhsT=codes[:, cols].bitcast(FP8X4),
-                        lhsT_scale=scales[:, cols],
-                        rhs=w_codes[:, 0:QK_COLS].bitcast(FP8X4),
-                        rhs_scale=w_scales[:, 0:QK_COLS],
-                        start=True,
-                        stop=True,
-                    )
-                    nc.tensor.matmul_mx(
-                        out=v_ps[:, cols],
-                        lhsT=codes[:, cols].bitcast(FP8X4),
-                        lhsT_scale=scales[:, cols],
-                        rhs=w_codes[:, QK_COLS : QK_COLS + V_COLS].bitcast(FP8X4),
-                        rhs_scale=w_scales[:, QK_COLS : QK_COLS + V_COLS],
-                        start=True,
-                        stop=True,
-                    )
-                banks.append(qk_ps)
-            qk_banks[i] = banks
-            v_banks[i] = v_ps
+            nc.vector.quantize_mx(
+                out=codes[:, pr_lo * 256 : pr_hi * 256].bitcast(FP8X4),
+                scales=scales[:, pr_lo * 256 : pr_hi * 256],
+                in_=grouped_tiles[i][:, pr_lo * 1024 : pr_hi * 1024],
+            )
+
+        def project_pair(i, pr):
+            codes, scales = code_tiles[i]
+            if pr == 0:
+                v_ps = ps_v.tile([P, 512], F32, name="v_ps", tag="v_ps")
+                v_banks[i] = v_ps
+            v_ps = v_banks[i]
+            qk_ps = ps_qk.tile([P, 512], F32, name="qk_ps", tag="qk_ps")
+            for j in range(2):
+                tl = 2 * pr + j
+                cols = slice(tl * P, (tl + 1) * P)
+                nc.tensor.matmul_mx(
+                    out=qk_ps[:, j * QK_COLS : (j + 1) * QK_COLS],
+                    lhsT=codes[:, cols].bitcast(FP8X4),
+                    lhsT_scale=scales[:, cols],
+                    rhs=w_codes[:, 0:QK_COLS].bitcast(FP8X4),
+                    rhs_scale=w_scales[:, 0:QK_COLS],
+                    start=True,
+                    stop=True,
+                )
+                nc.tensor.matmul_mx(
+                    out=v_ps[:, cols],
+                    lhsT=codes[:, cols].bitcast(FP8X4),
+                    lhsT_scale=scales[:, cols],
+                    rhs=w_codes[:, QK_COLS : QK_COLS + V_COLS].bitcast(FP8X4),
+                    rhs_scale=w_scales[:, QK_COLS : QK_COLS + V_COLS],
+                    start=True,
+                    stop=True,
+                )
+            qk_banks[i, pr] = qk_ps
 
         def rope_products(i, pr):
             gg = i % GROUPS_PER_BATCH
@@ -149,7 +150,7 @@ def tile_attention_pa_t_kernel(tc, hidden_states, cos, sin, w_qkv, out_0, out_1,
                 prod_tiles[i] = (pa, pb)
             pa, pb = prod_tiles[i]
             t0 = gg * TILES + 2 * pr
-            bank = qk_banks[i][pr][:].rearrange("p (j h d) -> p j h d", j=2, d=HEAD)
+            bank = qk_banks[i, pr][:].rearrange("p (j h d) -> p j h d", j=2, d=HEAD)
             pa_v = pa[:].rearrange("p (t h d) -> p t h d", t=TILES, d=HEAD)[:, 2 * pr : 2 * pr + 2, :, :]
             pb_v = pb[:].rearrange("p (t h d) -> p t h d", t=TILES, d=HEAD)[:, 2 * pr : 2 * pr + 2, :, :]
             nc.vector.tensor_tensor(
@@ -184,34 +185,32 @@ def tile_attention_pa_t_kernel(tc, hidden_states, cos, sin, w_qkv, out_0, out_1,
                 op=ADD,
             )
 
-        def copy_v(i):
+        def copy_and_store_v(i):
+            b, gg = divmod(i, GROUPS_PER_BATCH)
             v_out = opool.tile([P, TILES * P], F32, name="v_out", tag="v_out")
             nc.scalar.copy(out=v_out[:], in_=v_banks[i][:])
-            return v_out
+            nc.sync.dma_start(
+                out=vv[b, :, gg * TILES : (gg + 1) * TILES, :],
+                in_=v_out[:].rearrange("p (t c) -> p t c", c=P),
+            )
 
-        def store_group(i, v_out):
+        def store_qk(i, t_lo, t_hi):
             b, gg = divmod(i, GROUPS_PER_BATCH)
-            ts = slice(gg * TILES, (gg + 1) * TILES)
-            qk_out = out_tiles[i]
-            nc.sync.dma_start(out=vv[b, :, ts, :], in_=v_out[:].rearrange("p (t c) -> p t c", c=P))
-            nc.sync.dma_start(
-                out=qv[b, :, ts, :], in_=qk_out[:, 0 : TILES * P].rearrange("p (t c) -> p t c", c=P)
-            )
-            nc.sync.dma_start(
-                out=kv[b, :, ts, :],
-                in_=qk_out[:, TILES * P : 2 * TILES * P].rearrange("p (t c) -> p t c", c=P),
-            )
+            ts = slice(gg * TILES + t_lo, gg * TILES + t_hi)
+            qk_v = out_tiles[i][:].rearrange("p (g t c) -> p g t c", g=2, c=P)
+            nc.sync.dma_start(out=qv[b, :, ts, :], in_=qk_v[:, 0, t_lo:t_hi, :])
+            nc.sync.dma_start(out=kv[b, :, ts, :], in_=qk_v[:, 1, t_lo:t_hi, :])
 
-        load_x(0)
         nc.sync.dma_start(
             out=w_raw[:].rearrange("q (u f) -> q u f", u=2),
             in_=w_qkv.rearrange("(u q e) c -> q u (e c)", u=2, e=2),
         )
-        load_x(1)
+        load_x(0, 0, 2)
+        load_x(0, 2, TILES)
         nc.sync.dma_start(out=cos_v, in_=cos.rearrange("(p t) d -> p t d", t=T_PER_PART))
         nc.sync.dma_start(out=sin_v, in_=sin.rearrange("(p t) d -> p t d", t=T_PER_PART))
-        for i in range(2, N_GROUPS):
-            load_x(i)
+        for i in range(1, N_GROUPS):
+            load_x(i, 0, TILES)
 
         nc.vector.tensor_copy(
             out=w_grp[:].rearrange("p (c t) -> p c t", t=4),
@@ -228,32 +227,46 @@ def tile_attention_pa_t_kernel(tc, hidden_states, cos, sin, w_qkv, out_0, out_1,
             in_=w_grp[:, 4 * QK_COLS : 4 * (QK_COLS + V_COLS)],
         )
 
-        transpose_group(0)
-        copy_group(0)
-        quantise_group(0)
-        transpose_group(1)
-        copy_group(1)
-        quantise_group(1)
+        for pr in range(2):
+            transpose_pair(0, pr)
+            copy_pair(0, pr)
+            quantise(0, pr, pr + 1)
+        for pr in range(2):
+            project_pair(0, pr)
+            transpose_pair(1, pr)
+            copy_pair(1, pr)
         nc.vector.tensor_scalar_mul(out=sin_v[:, :, 0:HALF], in0=sin_v[:, :, 0:HALF], scalar1=-1.0)
-        project_group(0)
 
         for i in range(N_GROUPS):
             if i + 2 < N_GROUPS:
-                transpose_group(i + 2)
-            v_out = copy_v(i)
+                transpose_pair(i + 2, 0)
+                transpose_pair(i + 2, 1)
+            copy_and_store_v(i)
             if i + 2 < N_GROUPS:
-                copy_group(i + 2)
+                copy_pair(i + 2, 0)
+                copy_pair(i + 2, 1)
+            if i == 0:
+                rope_products(0, 0)
+                rope_products(0, 1)
+                quantise(1, 0, 2)
+                project_pair(1, 0)
+                project_pair(1, 1)
+                quantise(2, 0, 2)
+                rope_sum(0, nc.gpsimd, 0, TILES)
+                store_qk(0, 0, TILES)
+                continue
             if i + 1 < N_GROUPS:
-                project_group(i + 1)
-            if i + 1 < N_GROUPS:
+                project_pair(i + 1, 0)
+                project_pair(i + 1, 1)
+            if i < N_GROUPS - 2:
                 rope_products(i, 0)
                 rope_products(i, 1)
-                if i + 2 < N_GROUPS:
-                    quantise_group(i + 2)
+                quantise(i + 2, 0, 2)
                 rope_sum(i, nc.gpsimd, 0, TILES)
+                store_qk(i, 0, TILES)
             else:
-                rope_products(i, 0)
-                rope_sum(i, nc.gpsimd, 0, 2)
-                rope_products(i, 1)
-                rope_sum(i, nc.vector, 2, TILES)
-            store_group(i, v_out)
+                engine = nc.gpsimd if i == N_GROUPS - 2 else nc.vector
+                for pr in range(2):
+                    rope_products(i, pr)
+                    rope_sum(i, engine, 2 * pr, 2 * pr + 2)
+                    store_qk(i, 2 * pr, 2 * pr + 2)

@@ -19,6 +19,7 @@ HEAD = 64
 HALF = 32
 QK_COLS = 256
 V_COLS = 128
+W_COLS = 2 * QK_COLS + V_COLS
 T_PER_PART = SEQ // P
 TILES = 4
 GROUPS_PER_BATCH = T_PER_PART // TILES
@@ -59,13 +60,13 @@ def tile_attention_pa_t_kernel(tc, hidden_states, cos, sin, w_qkv, out_0, out_1,
         make_identity(nc, ident[:])
 
         w_raw = const.tile([P, 4 * (QK_COLS + V_COLS)], BF16, name="w_raw")
-        w_grp = const.tile([P, 4 * (QK_COLS + V_COLS)], BF16, name="w_grp", align_bytes=64)
-        w_codes = const.tile([P, QK_COLS + V_COLS], U32, name="w_codes", align_bytes=64)
-        w_scales = const.tile([P, QK_COLS + V_COLS], U8, name="w_scales", align_bytes=64)
-        cos_sb = const.tile([P, T_PER_PART * HEAD], BF16, name="cos_sb")
-        sin_sb = const.tile([P, T_PER_PART * HEAD], BF16, name="sin_sb")
-        cos_v = cos_sb[:].rearrange("p (t d) -> p t d", d=HEAD)
-        sin_v = sin_sb[:].rearrange("p (t d) -> p t d", d=HEAD)
+        w_grp = const.tile([P, 4 * W_COLS], BF16, name="w_grp", align_bytes=64)
+        w_codes = const.tile([P, W_COLS], U32, name="w_codes", align_bytes=64)
+        w_scales = const.tile([P, W_COLS], U8, name="w_scales", align_bytes=64)
+        table = const.tile([P, 2 * T_PER_PART * HEAD], BF16, name="table")
+        table_v = table[:].rearrange("p (s t d) -> p s t d", s=2, d=HEAD)
+        cos_v = table_v[:, 0, :, :]
+        sin_v = table_v[:, 1, :, :]
 
         def load_x(i, t_lo, t_hi):
             b, gg = divmod(i, GROUPS_PER_BATCH)
@@ -112,76 +113,56 @@ def tile_attention_pa_t_kernel(tc, hidden_states, cos, sin, w_qkv, out_0, out_1,
                 in_=grouped_tiles[i][:, pr_lo * 1024 : pr_hi * 1024],
             )
 
-        def project_pair(i, pr):
+        def project_tile(i, tl):
             codes, scales = code_tiles[i]
-            if pr == 0:
+            if tl == 0:
                 v_ps = ps_v.tile([P, 512], F32, name="v_ps", tag="v_ps")
                 v_banks[i] = v_ps
             v_ps = v_banks[i]
             qk_ps = ps_qk.tile([P, 512], F32, name="qk_ps", tag="qk_ps")
-            for j in range(2):
-                tl = 2 * pr + j
-                cols = slice(tl * P, (tl + 1) * P)
-                nc.tensor.matmul_mx(
-                    out=qk_ps[:, j * QK_COLS : (j + 1) * QK_COLS],
-                    lhsT=codes[:, cols].bitcast(FP8X4),
-                    lhsT_scale=scales[:, cols],
-                    rhs=w_codes[:, 0:QK_COLS].bitcast(FP8X4),
-                    rhs_scale=w_scales[:, 0:QK_COLS],
-                    start=True,
-                    stop=True,
-                )
-                nc.tensor.matmul_mx(
-                    out=v_ps[:, cols],
-                    lhsT=codes[:, cols].bitcast(FP8X4),
-                    lhsT_scale=scales[:, cols],
-                    rhs=w_codes[:, QK_COLS : QK_COLS + V_COLS].bitcast(FP8X4),
-                    rhs_scale=w_scales[:, QK_COLS : QK_COLS + V_COLS],
-                    start=True,
-                    stop=True,
-                )
-            qk_banks[i, pr] = qk_ps
+            cols = slice(tl * P, (tl + 1) * P)
+            nc.tensor.matmul_mx(
+                out=qk_ps[:],
+                lhsT=codes[:, cols].bitcast(FP8X4),
+                lhsT_scale=scales[:, cols],
+                rhs=w_codes[:, 0 : 2 * QK_COLS].bitcast(FP8X4),
+                rhs_scale=w_scales[:, 0 : 2 * QK_COLS],
+                start=True,
+                stop=True,
+            )
+            nc.tensor.matmul_mx(
+                out=v_ps[:, cols],
+                lhsT=codes[:, cols].bitcast(FP8X4),
+                lhsT_scale=scales[:, cols],
+                rhs=w_codes[:, 2 * QK_COLS : W_COLS].bitcast(FP8X4),
+                rhs_scale=w_scales[:, 2 * QK_COLS : W_COLS],
+                start=True,
+                stop=True,
+            )
+            qk_banks[i, tl] = qk_ps
 
-        def rope_products(i, pr):
-            gg = i % GROUPS_PER_BATCH
-            if pr == 0:
-                pa = rpool.tile([P, TILES * QK_COLS], F32, name="pa", tag="pa")
-                pb = rpool.tile([P, TILES * QK_COLS], F32, name="pb", tag="pb")
-                prod_tiles[i] = (pa, pb)
-            pa, pb = prod_tiles[i]
-            t0 = gg * TILES + 2 * pr
-            bank = qk_banks[i, pr][:].rearrange("p (j h d) -> p j h d", j=2, d=HEAD)
-            pa_v = pa[:].rearrange("p (t h d) -> p t h d", t=TILES, d=HEAD)[:, 2 * pr : 2 * pr + 2, :, :]
-            pb_v = pb[:].rearrange("p (t h d) -> p t h d", t=TILES, d=HEAD)[:, 2 * pr : 2 * pr + 2, :, :]
+        def rope_products(i, tl):
+            if tl == 0:
+                prod = rpool.tile([P, TILES * 2 * QK_COLS], F32, name="prod", tag="prod")
+                prod_tiles[i] = prod
+            t = (i % GROUPS_PER_BATCH) * TILES + tl
             nc.vector.tensor_tensor(
-                out=pa_v,
-                in0=bank,
-                in1=cos_v[:, t0 : t0 + 2, :].unsqueeze(2).to_broadcast([P, 2, 4, HEAD]),
-                op=MULT,
-            )
-            nc.vector.tensor_tensor(
-                out=pb_v[:, :, :, 0:HALF],
-                in0=bank[:, :, :, HALF:HEAD],
-                in1=sin_v[:, t0 : t0 + 2, 0:HALF].unsqueeze(2).to_broadcast([P, 2, 4, HALF]),
-                op=MULT,
-            )
-            nc.vector.tensor_tensor(
-                out=pb_v[:, :, :, HALF:HEAD],
-                in0=bank[:, :, :, 0:HALF],
-                in1=sin_v[:, t0 : t0 + 2, HALF:HEAD].unsqueeze(2).to_broadcast([P, 2, 4, HALF]),
+                out=prod_tiles[i][:, tl * 512 : (tl + 1) * 512].rearrange("p (s h d) -> p s h d", s=2, d=HEAD),
+                in0=qk_banks[i, tl][:].rearrange("p (s h d) -> p s h d", s=2, d=HEAD),
+                in1=table_v[:, :, t, :].unsqueeze(2).to_broadcast([P, 2, 4, HEAD]),
                 op=MULT,
             )
 
         def rope_sum(i, engine, t_lo, t_hi):
-            pa, pb = prod_tiles[i]
+            prod_v = prod_tiles[i][:].rearrange("p (t s g c) -> p t s g c", s=2, g=2, c=P)
             if i not in out_tiles:
                 qk_out = opool.tile([P, 2 * TILES * P], F32, name="qk_out", tag="qk_out")
                 out_tiles[i] = qk_out
             qk_out = out_tiles[i]
             engine.tensor_tensor(
                 out=qk_out[:].rearrange("p (g t c) -> p t g c", g=2, c=P)[:, t_lo:t_hi, :, :],
-                in0=pa[:].rearrange("p (t g c) -> p t g c", g=2, c=P)[:, t_lo:t_hi, :, :],
-                in1=pb[:].rearrange("p (t g c) -> p t g c", g=2, c=P)[:, t_lo:t_hi, :, :],
+                in0=prod_v[:, t_lo:t_hi, 0, :, :],
+                in1=prod_v[:, t_lo:t_hi, 1, :, :],
                 op=ADD,
             )
 
@@ -201,72 +182,66 @@ def tile_attention_pa_t_kernel(tc, hidden_states, cos, sin, w_qkv, out_0, out_1,
             nc.sync.dma_start(out=qv[b, :, ts, :], in_=qk_v[:, 0, t_lo:t_hi, :])
             nc.sync.dma_start(out=kv[b, :, ts, :], in_=qk_v[:, 1, t_lo:t_hi, :])
 
+        load_x(0, 0, TILES)
         nc.sync.dma_start(
             out=w_raw[:].rearrange("q (u f) -> q u f", u=2),
             in_=w_qkv.rearrange("(u q e) c -> q u (e c)", u=2, e=2),
         )
-        load_x(0, 0, 2)
-        load_x(0, 2, TILES)
+        load_x(1, 0, TILES)
         nc.sync.dma_start(out=cos_v, in_=cos.rearrange("(p t) d -> p t d", t=T_PER_PART))
         nc.sync.dma_start(out=sin_v, in_=sin.rearrange("(p t) d -> p t d", t=T_PER_PART))
-        for i in range(1, N_GROUPS):
+        for i in range(2, N_GROUPS):
             load_x(i, 0, TILES)
-
-        nc.vector.tensor_copy(
-            out=w_grp[:].rearrange("p (c t) -> p c t", t=4),
-            in_=w_raw[:].rearrange("p (t c) -> p c t", t=4),
-        )
-        nc.vector.quantize_mx(
-            out=w_codes[:, 0:QK_COLS].bitcast(FP8X4),
-            scales=w_scales[:, 0:QK_COLS],
-            in_=w_grp[:, 0 : 4 * QK_COLS],
-        )
-        nc.vector.quantize_mx(
-            out=w_codes[:, QK_COLS : QK_COLS + V_COLS].bitcast(FP8X4),
-            scales=w_scales[:, QK_COLS : QK_COLS + V_COLS],
-            in_=w_grp[:, 4 * QK_COLS : 4 * (QK_COLS + V_COLS)],
-        )
 
         for pr in range(2):
             transpose_pair(0, pr)
-            copy_pair(0, pr)
-            quantise(0, pr, pr + 1)
         for pr in range(2):
-            project_pair(0, pr)
+            copy_pair(0, pr)
+        w_src = w_raw[:].rearrange("p (t h f d) -> p h f d t", t=4, f=2, d=HALF)
+        w_dst = w_grp[:].rearrange("p (h f d t) -> p h f d t", f=2, d=HALF, t=4)
+        nc.vector.tensor_copy(out=w_dst[:, 0:4, :, :, :], in_=w_src[:, 0:4, :, :, :])
+        for f in range(2):
+            nc.vector.tensor_copy(out=w_dst[:, 4:8, f, :, :], in_=w_src[:, 0:4, 1 - f, :, :])
+        nc.vector.tensor_copy(out=w_dst[:, 8:10, :, :, :], in_=w_src[:, 4:6, :, :, :])
+        quantise(0, 0, 2)
+        nc.vector.quantize_mx(
+            out=w_codes[:, 0 : 2 * QK_COLS].bitcast(FP8X4),
+            scales=w_scales[:, 0 : 2 * QK_COLS],
+            in_=w_grp[:, 0 : 8 * QK_COLS],
+        )
+        nc.vector.quantize_mx(
+            out=w_codes[:, 2 * QK_COLS : W_COLS].bitcast(FP8X4),
+            scales=w_scales[:, 2 * QK_COLS : W_COLS],
+            in_=w_grp[:, 8 * QK_COLS : 4 * W_COLS],
+        )
+        for pr in range(2):
             transpose_pair(1, pr)
+        for pr in range(2):
             copy_pair(1, pr)
+        quantise(1, 0, 2)
         nc.vector.tensor_scalar_mul(out=sin_v[:, :, 0:HALF], in0=sin_v[:, :, 0:HALF], scalar1=-1.0)
+        project_tile(0, 0)
+        project_tile(0, 1)
 
         for i in range(N_GROUPS):
+            last = i == N_GROUPS - 1
             if i + 2 < N_GROUPS:
-                transpose_pair(i + 2, 0)
-                transpose_pair(i + 2, 1)
+                for pr in range(2):
+                    transpose_pair(i + 2, pr)
+                for pr in range(2):
+                    copy_pair(i + 2, pr)
+            for tl in range(TILES):
+                rope_products(i, tl)
+                ahead = i * TILES + tl + 2
+                if ahead < N_GROUPS * TILES:
+                    project_tile(ahead // TILES, ahead % TILES)
+                if last and tl == 1:
+                    rope_sum(i, nc.gpsimd, 0, 2)
             copy_and_store_v(i)
             if i + 2 < N_GROUPS:
-                copy_pair(i + 2, 0)
-                copy_pair(i + 2, 1)
-            if i == 0:
-                rope_products(0, 0)
-                rope_products(0, 1)
-                quantise(1, 0, 2)
-                project_pair(1, 0)
-                project_pair(1, 1)
-                quantise(2, 0, 2)
-                rope_sum(0, nc.gpsimd, 0, TILES)
-                store_qk(0, 0, TILES)
-                continue
-            if i + 1 < N_GROUPS:
-                project_pair(i + 1, 0)
-                project_pair(i + 1, 1)
-            if i < N_GROUPS - 2:
-                rope_products(i, 0)
-                rope_products(i, 1)
                 quantise(i + 2, 0, 2)
-                rope_sum(i, nc.gpsimd, 0, TILES)
-                store_qk(i, 0, TILES)
+            if last:
+                rope_sum(i, nc.vector, 2, TILES)
             else:
-                engine = nc.gpsimd if i == N_GROUPS - 2 else nc.vector
-                for pr in range(2):
-                    rope_products(i, pr)
-                    rope_sum(i, engine, 2 * pr, 2 * pr + 2)
-                    store_qk(i, 2 * pr, 2 * pr + 2)
+                rope_sum(i, nc.gpsimd, 0, TILES)
+            store_qk(i, 0, TILES)

@@ -19,7 +19,6 @@ HEAD = 64
 HALF = 32
 QK_COLS = 256
 V_COLS = 128
-W_COLS = 2 * QK_COLS + V_COLS
 T_PER_PART = SEQ // P
 TILES = 4
 GROUPS_PER_BATCH = T_PER_PART // TILES
@@ -60,120 +59,140 @@ def tile_attention_pa_t_kernel(tc, hidden_states, cos, sin, w_qkv, out_0, out_1,
         make_identity(nc, ident[:])
 
         w_raw = const.tile([P, 4 * (QK_COLS + V_COLS)], BF16, name="w_raw")
-        w_grp = const.tile([P, 4 * W_COLS], BF16, name="w_grp", align_bytes=64)
-        w_codes = const.tile([P, W_COLS], U32, name="w_codes", align_bytes=64)
-        w_scales = const.tile([P, W_COLS], U8, name="w_scales", align_bytes=64)
-        table = const.tile([P, 2 * T_PER_PART * HEAD], BF16, name="table")
-        table_v = table[:].rearrange("p (s t d) -> p s t d", s=2, d=HEAD)
-        cos_v = table_v[:, 0, :, :]
-        sin_v = table_v[:, 1, :, :]
+        w_grp = const.tile([P, 4 * (QK_COLS + V_COLS)], BF16, name="w_grp", align_bytes=64)
+        w_codes = const.tile([P, QK_COLS + V_COLS], U32, name="w_codes", align_bytes=64)
+        w_scales = const.tile([P, QK_COLS + V_COLS], U8, name="w_scales", align_bytes=64)
+        cos_sb = const.tile([P, T_PER_PART * HEAD], BF16, name="cos_sb")
+        sin_sb = const.tile([P, T_PER_PART * HEAD], BF16, name="sin_sb")
+        cos_v = cos_sb[:].rearrange("p (t d) -> p t d", d=HEAD)
+        sin_v = sin_sb[:].rearrange("p (t d) -> p t d", d=HEAD)
 
-        def load_x(i, t_lo, t_hi):
+        def load_x(i):
             b, gg = divmod(i, GROUPS_PER_BATCH)
-            if i not in x_tiles:
-                x_sb = xpool.tile([P, TILES * HID], BF16, name="x_sb", tag="x_sb")
-                x_tiles[i] = x_sb
+            x_sb = xpool.tile([P, TILES * HID], BF16, name="x_sb", tag="x_sb")
             nc.sync.dma_start(
-                out=x_tiles[i][:, t_lo * HID : t_hi * HID].rearrange("p (t k) -> p t k", k=HID),
-                in_=xv[b, :, gg * TILES + t_lo : gg * TILES + t_hi, :],
+                out=x_sb[:].rearrange("p (t k) -> p t k", k=HID),
+                in_=xv[b, :, gg * TILES : (gg + 1) * TILES, :],
             )
+            x_tiles[i] = x_sb
 
-        def transpose_pair(i, pr):
+        def transpose_group(i):
             words = x_tiles[i][:].bitcast(F32)
-            xt = ps_x.tile([P, 512], F32, name="xt", tag="xt")
-            for j in range(2):
-                for u in range(2):
-                    col = (2 * pr + j) * 256 + u * P
-                    nc.tensor.transpose(
-                        xt[:, u * 256 + j * P : u * 256 + (j + 1) * P],
-                        words[:, col : col + P],
-                        ident[:],
-                    )
-            xt_tiles[i, pr] = xt
+            banks = []
+            for pr in range(2):
+                xt = ps_x.tile([P, 512], F32, name="xt", tag="xt")
+                for j in range(2):
+                    for u in range(2):
+                        col = (2 * pr + j) * 256 + u * P
+                        nc.tensor.transpose(
+                            xt[:, u * 256 + j * P : u * 256 + (j + 1) * P],
+                            words[:, col : col + P],
+                            ident[:],
+                        )
+                banks.append(xt)
+            xt_tiles[i] = banks
 
-        def copy_pair(i, pr):
-            if pr == 0:
-                grouped = gpool.tile([P, TILES * HID], BF16, name="grouped", tag="grouped", align_bytes=64)
-                grouped_tiles[i] = grouped
-            gw = grouped_tiles[i][:].bitcast(F32)
-            nc.scalar.copy(
-                out=gw[:, pr * 512 : (pr + 1) * 512].rearrange("p (m u) -> p m u", u=2),
-                in_=xt_tiles[i, pr][:].rearrange("p (u m) -> p m u", u=2),
-            )
+        def copy_group(i):
+            grouped = gpool.tile([P, TILES * HID], BF16, name="grouped", tag="grouped", align_bytes=64)
+            gw = grouped[:].bitcast(F32)
+            for pr in range(2):
+                nc.scalar.copy(
+                    out=gw[:, pr * 512 : (pr + 1) * 512].rearrange("p (m u) -> p m u", u=2),
+                    in_=xt_tiles[i][pr][:].rearrange("p (u m) -> p m u", u=2),
+                )
+            grouped_tiles[i] = grouped
 
-        def quantise(i, pr_lo, pr_hi):
-            if pr_lo == 0:
-                codes = cpool.tile([P, TILES * P], U32, name="codes", tag="codes", align_bytes=64)
-                scales = cpool.tile([P, TILES * P], U8, name="scales", tag="scales", align_bytes=64)
-                code_tiles[i] = (codes, scales)
-            codes, scales = code_tiles[i]
+        def quantise_group(i):
+            codes = cpool.tile([P, TILES * P], U32, name="codes", tag="codes", align_bytes=64)
+            scales = cpool.tile([P, TILES * P], U8, name="scales", tag="scales", align_bytes=64)
             nc.vector.quantize_mx(
-                out=codes[:, pr_lo * 256 : pr_hi * 256].bitcast(FP8X4),
-                scales=scales[:, pr_lo * 256 : pr_hi * 256],
-                in_=grouped_tiles[i][:, pr_lo * 1024 : pr_hi * 1024],
+                out=codes[:].bitcast(FP8X4), scales=scales[:], in_=grouped_tiles[i][:]
             )
+            code_tiles[i] = (codes, scales)
 
-        def project_tile(i, tl):
+        def project_group(i):
             codes, scales = code_tiles[i]
-            if tl == 0:
-                v_ps = ps_v.tile([P, 512], F32, name="v_ps", tag="v_ps")
-                v_banks[i] = v_ps
-            v_ps = v_banks[i]
-            qk_ps = ps_qk.tile([P, 512], F32, name="qk_ps", tag="qk_ps")
-            cols = slice(tl * P, (tl + 1) * P)
-            nc.tensor.matmul_mx(
-                out=qk_ps[:],
-                lhsT=codes[:, cols].bitcast(FP8X4),
-                lhsT_scale=scales[:, cols],
-                rhs=w_codes[:, 0 : 2 * QK_COLS].bitcast(FP8X4),
-                rhs_scale=w_scales[:, 0 : 2 * QK_COLS],
-                start=True,
-                stop=True,
-            )
-            nc.tensor.matmul_mx(
-                out=v_ps[:, cols],
-                lhsT=codes[:, cols].bitcast(FP8X4),
-                lhsT_scale=scales[:, cols],
-                rhs=w_codes[:, 2 * QK_COLS : W_COLS].bitcast(FP8X4),
-                rhs_scale=w_scales[:, 2 * QK_COLS : W_COLS],
-                start=True,
-                stop=True,
-            )
-            qk_banks[i, tl] = qk_ps
+            v_ps = ps_v.tile([P, 512], F32, name="v_ps", tag="v_ps")
+            banks = []
+            for pr in range(2):
+                qk_ps = ps_qk.tile([P, 512], F32, name="qk_ps", tag="qk_ps")
+                for j in range(2):
+                    tl = 2 * pr + j
+                    cols = slice(tl * P, (tl + 1) * P)
+                    nc.tensor.matmul_mx(
+                        out=qk_ps[:, j * QK_COLS : (j + 1) * QK_COLS],
+                        lhsT=codes[:, cols].bitcast(FP8X4),
+                        lhsT_scale=scales[:, cols],
+                        rhs=w_codes[:, 0:QK_COLS].bitcast(FP8X4),
+                        rhs_scale=w_scales[:, 0:QK_COLS],
+                        start=True,
+                        stop=True,
+                    )
+                    nc.tensor.matmul_mx(
+                        out=v_ps[:, cols],
+                        lhsT=codes[:, cols].bitcast(FP8X4),
+                        lhsT_scale=scales[:, cols],
+                        rhs=w_codes[:, QK_COLS : QK_COLS + V_COLS].bitcast(FP8X4),
+                        rhs_scale=w_scales[:, QK_COLS : QK_COLS + V_COLS],
+                        start=True,
+                        stop=True,
+                    )
+                banks.append(qk_ps)
+            qk_banks[i] = banks
+            v_banks[i] = v_ps
 
-        def rope_products(i, tl):
-            if tl == 0:
-                prod = rpool.tile([P, TILES * 2 * QK_COLS], F32, name="prod", tag="prod")
-                prod_tiles[i] = prod
-            t = (i % GROUPS_PER_BATCH) * TILES + tl
+        def rope_products(i, pr):
+            gg = i % GROUPS_PER_BATCH
+            if pr == 0:
+                pa = rpool.tile([P, TILES * QK_COLS], F32, name="pa", tag="pa")
+                pb = rpool.tile([P, TILES * QK_COLS], F32, name="pb", tag="pb")
+                prod_tiles[i] = (pa, pb)
+            pa, pb = prod_tiles[i]
+            t0 = gg * TILES + 2 * pr
+            bank = qk_banks[i][pr][:].rearrange("p (j h d) -> p j h d", j=2, d=HEAD)
+            pa_v = pa[:].rearrange("p (t h d) -> p t h d", t=TILES, d=HEAD)[:, 2 * pr : 2 * pr + 2, :, :]
+            pb_v = pb[:].rearrange("p (t h d) -> p t h d", t=TILES, d=HEAD)[:, 2 * pr : 2 * pr + 2, :, :]
             nc.vector.tensor_tensor(
-                out=prod_tiles[i][:, tl * 512 : (tl + 1) * 512].rearrange("p (s h d) -> p s h d", s=2, d=HEAD),
-                in0=qk_banks[i, tl][:].rearrange("p (s h d) -> p s h d", s=2, d=HEAD),
-                in1=table_v[:, :, t, :].unsqueeze(2).to_broadcast([P, 2, 4, HEAD]),
+                out=pa_v,
+                in0=bank,
+                in1=cos_v[:, t0 : t0 + 2, :].unsqueeze(2).to_broadcast([P, 2, 4, HEAD]),
+                op=MULT,
+            )
+            nc.vector.tensor_tensor(
+                out=pb_v[:, :, :, 0:HALF],
+                in0=bank[:, :, :, HALF:HEAD],
+                in1=sin_v[:, t0 : t0 + 2, 0:HALF].unsqueeze(2).to_broadcast([P, 2, 4, HALF]),
+                op=MULT,
+            )
+            nc.vector.tensor_tensor(
+                out=pb_v[:, :, :, HALF:HEAD],
+                in0=bank[:, :, :, 0:HALF],
+                in1=sin_v[:, t0 : t0 + 2, HALF:HEAD].unsqueeze(2).to_broadcast([P, 2, 4, HALF]),
                 op=MULT,
             )
 
         def rope_sum(i, engine, t_lo, t_hi):
-            prod_v = prod_tiles[i][:].rearrange("p (t s g c) -> p t s g c", s=2, g=2, c=P)
+            pa, pb = prod_tiles[i]
             if i not in out_tiles:
                 qk_out = opool.tile([P, 2 * TILES * P], F32, name="qk_out", tag="qk_out")
                 out_tiles[i] = qk_out
             qk_out = out_tiles[i]
             engine.tensor_tensor(
                 out=qk_out[:].rearrange("p (g t c) -> p t g c", g=2, c=P)[:, t_lo:t_hi, :, :],
-                in0=prod_v[:, t_lo:t_hi, 0, :, :],
-                in1=prod_v[:, t_lo:t_hi, 1, :, :],
+                in0=pa[:].rearrange("p (t g c) -> p t g c", g=2, c=P)[:, t_lo:t_hi, :, :],
+                in1=pb[:].rearrange("p (t g c) -> p t g c", g=2, c=P)[:, t_lo:t_hi, :, :],
                 op=ADD,
             )
 
-        def copy_and_store_v(i):
-            b, gg = divmod(i, GROUPS_PER_BATCH)
+        def copy_v(i):
             v_out = opool.tile([P, TILES * P], F32, name="v_out", tag="v_out")
             nc.scalar.copy(out=v_out[:], in_=v_banks[i][:])
-            nc.sync.dma_start(
-                out=vv[b, :, gg * TILES : (gg + 1) * TILES, :],
-                in_=v_out[:].rearrange("p (t c) -> p t c", c=P),
-            )
+            return v_out
+
+        def store_v(i, v_out):
+            b, gg = divmod(i, GROUPS_PER_BATCH)
+            ts = slice(gg * TILES, (gg + 1) * TILES)
+            nc.sync.dma_start(out=vv[b, :, ts, :], in_=v_out[:].rearrange("p (t c) -> p t c", c=P))
 
         def store_qk(i, t_lo, t_hi):
             b, gg = divmod(i, GROUPS_PER_BATCH)
@@ -182,66 +201,60 @@ def tile_attention_pa_t_kernel(tc, hidden_states, cos, sin, w_qkv, out_0, out_1,
             nc.sync.dma_start(out=qv[b, :, ts, :], in_=qk_v[:, 0, t_lo:t_hi, :])
             nc.sync.dma_start(out=kv[b, :, ts, :], in_=qk_v[:, 1, t_lo:t_hi, :])
 
-        load_x(0, 0, TILES)
+        load_x(0)
         nc.sync.dma_start(
             out=w_raw[:].rearrange("q (u f) -> q u f", u=2),
             in_=w_qkv.rearrange("(u q e) c -> q u (e c)", u=2, e=2),
         )
-        load_x(1, 0, TILES)
+        load_x(1)
         nc.sync.dma_start(out=cos_v, in_=cos.rearrange("(p t) d -> p t d", t=T_PER_PART))
         nc.sync.dma_start(out=sin_v, in_=sin.rearrange("(p t) d -> p t d", t=T_PER_PART))
         for i in range(2, N_GROUPS):
-            load_x(i, 0, TILES)
+            load_x(i)
 
-        for pr in range(2):
-            transpose_pair(0, pr)
-        for pr in range(2):
-            copy_pair(0, pr)
-        w_src = w_raw[:].rearrange("p (t h f d) -> p h f d t", t=4, f=2, d=HALF)
-        w_dst = w_grp[:].rearrange("p (h f d t) -> p h f d t", f=2, d=HALF, t=4)
-        nc.vector.tensor_copy(out=w_dst[:, 0:4, :, :, :], in_=w_src[:, 0:4, :, :, :])
-        for f in range(2):
-            nc.vector.tensor_copy(out=w_dst[:, 4:8, f, :, :], in_=w_src[:, 0:4, 1 - f, :, :])
-        nc.vector.tensor_copy(out=w_dst[:, 8:10, :, :, :], in_=w_src[:, 4:6, :, :, :])
-        quantise(0, 0, 2)
-        nc.vector.quantize_mx(
-            out=w_codes[:, 0 : 2 * QK_COLS].bitcast(FP8X4),
-            scales=w_scales[:, 0 : 2 * QK_COLS],
-            in_=w_grp[:, 0 : 8 * QK_COLS],
+        nc.vector.tensor_copy(
+            out=w_grp[:].rearrange("p (c t) -> p c t", t=4),
+            in_=w_raw[:].rearrange("p (t c) -> p c t", t=4),
         )
         nc.vector.quantize_mx(
-            out=w_codes[:, 2 * QK_COLS : W_COLS].bitcast(FP8X4),
-            scales=w_scales[:, 2 * QK_COLS : W_COLS],
-            in_=w_grp[:, 8 * QK_COLS : 4 * W_COLS],
+            out=w_codes[:, 0:QK_COLS].bitcast(FP8X4),
+            scales=w_scales[:, 0:QK_COLS],
+            in_=w_grp[:, 0 : 4 * QK_COLS],
         )
-        for pr in range(2):
-            transpose_pair(1, pr)
-        for pr in range(2):
-            copy_pair(1, pr)
-        quantise(1, 0, 2)
+        nc.vector.quantize_mx(
+            out=w_codes[:, QK_COLS : QK_COLS + V_COLS].bitcast(FP8X4),
+            scales=w_scales[:, QK_COLS : QK_COLS + V_COLS],
+            in_=w_grp[:, 4 * QK_COLS : 4 * (QK_COLS + V_COLS)],
+        )
+
+        transpose_group(0)
+        copy_group(0)
+        quantise_group(0)
+        transpose_group(1)
+        copy_group(1)
+        quantise_group(1)
         nc.vector.tensor_scalar_mul(out=sin_v[:, :, 0:HALF], in0=sin_v[:, :, 0:HALF], scalar1=-1.0)
-        project_tile(0, 0)
-        project_tile(0, 1)
+        project_group(0)
 
         for i in range(N_GROUPS):
-            last = i == N_GROUPS - 1
             if i + 2 < N_GROUPS:
-                for pr in range(2):
-                    transpose_pair(i + 2, pr)
-                for pr in range(2):
-                    copy_pair(i + 2, pr)
-            for tl in range(TILES):
-                rope_products(i, tl)
-                ahead = i * TILES + tl + 2
-                if ahead < N_GROUPS * TILES:
-                    project_tile(ahead // TILES, ahead % TILES)
-                if last and tl == 1:
-                    rope_sum(i, nc.gpsimd, 0, 2)
-            copy_and_store_v(i)
+                transpose_group(i + 2)
+            v_out = copy_v(i)
             if i + 2 < N_GROUPS:
-                quantise(i + 2, 0, 2)
-            if last:
-                rope_sum(i, nc.vector, 2, TILES)
-            else:
+                copy_group(i + 2)
+            if i + 1 < N_GROUPS:
+                project_group(i + 1)
+            if i + 1 < N_GROUPS:
+                rope_products(i, 0)
+                rope_products(i, 1)
+                if i + 2 < N_GROUPS:
+                    quantise_group(i + 2)
                 rope_sum(i, nc.gpsimd, 0, TILES)
-            store_qk(i, 0, TILES)
+                store_v(i, v_out)
+                store_qk(i, 0, TILES)
+            else:
+                store_v(i, v_out)
+                for pr in range(2):
+                    rope_products(i, pr)
+                    rope_sum(i, nc.vector, 2 * pr, 2 * pr + 2)
+                    store_qk(i, 2 * pr, 2 * pr + 2)

from contextlib import ExitStack

import concourse.mybir as mybir
from concourse.masks import make_identity

F32 = mybir.dt.float32
BF16 = mybir.dt.bfloat16
U32 = mybir.dt.uint32
U8 = mybir.dt.uint8
FP8X4 = mybir.dt.float8_e4m3fn_x4
MULT = mybir.AluOpType.mult
ADD = mybir.AluOpType.add

P = 128
BATCH = 4
SEQ = 2048
HID = 512
HEAD = 64
HALF = 32
QK_COLS = 256
V_COLS = 128
T_PER_PART = SEQ // P
TILES = 4
GROUPS_PER_BATCH = T_PER_PART // TILES
N_GROUPS = BATCH * GROUPS_PER_BATCH

FLOPS = 2 * BATCH * SEQ * HID * (QK_COLS + V_COLS)


def tile_attention_pa_t_kernel(tc, hidden_states, cos, sin, w_qkv, out_0, out_1, out_2):
    nc = tc.nc
    xv = hidden_states.rearrange("b (p t) k -> b p t k", t=T_PER_PART)
    qv = out_0.rearrange("b (p t) h d -> b p t (h d)", t=T_PER_PART)
    kv = out_1.rearrange("b (p t) h d -> b p t (h d)", t=T_PER_PART)
    vv = out_2.rearrange("b (p t) h d -> b p t (h d)", t=T_PER_PART)

    with ExitStack() as ctx:
        const = ctx.enter_context(tc.tile_pool(name="const", bufs=1))
        xpool = ctx.enter_context(tc.tile_pool(name="xpool", bufs=N_GROUPS))
        gpool = ctx.enter_context(tc.tile_pool(name="gpool", bufs=3))
        cpool = ctx.enter_context(tc.tile_pool(name="cpool", bufs=3))
        rpool = ctx.enter_context(tc.tile_pool(name="rpool", bufs=3))
        opool = ctx.enter_context(tc.tile_pool(name="opool", bufs=N_GROUPS))
        ps_x = ctx.enter_context(tc.psum_pool(name="ps_x", bufs=2))
        ps_qk = ctx.enter_context(tc.psum_pool(name="ps_qk", bufs=4))
        ps_v = ctx.enter_context(tc.psum_pool(name="ps_v", bufs=2))
        ctx.enter_context(tc.manual_schedule())

        x_tiles = {}
        xt_tiles = {}
        grouped_tiles = {}
        code_tiles = {}
        qk_banks = {}
        v_banks = {}
        prod_tiles = {}
        out_tiles = {}

        ident = const.tile([P, P], F32, name="ident")
        make_identity(nc, ident[:])

        w_raw = const.tile([P, 4 * (QK_COLS + V_COLS)], BF16, name="w_raw")
        w_grp = const.tile([P, 4 * (QK_COLS + V_COLS)], BF16, name="w_grp", align_bytes=64)
        w_codes = const.tile([P, QK_COLS + V_COLS], U32, name="w_codes", align_bytes=64)
        w_scales = const.tile([P, QK_COLS + V_COLS], U8, name="w_scales", align_bytes=64)
        cos_sb = const.tile([P, T_PER_PART * HEAD], BF16, name="cos_sb")
        sin_sb = const.tile([P, T_PER_PART * HEAD], BF16, name="sin_sb")
        cos_v = cos_sb[:].rearrange("p (t d) -> p t d", d=HEAD)
        sin_v = sin_sb[:].rearrange("p (t d) -> p t d", d=HEAD)

        def load_x(i):
            b, gg = divmod(i, GROUPS_PER_BATCH)
            x_sb = xpool.tile([P, TILES * HID], BF16, name="x_sb", tag="x_sb")
            nc.sync.dma_start(
                out=x_sb[:].rearrange("p (t k) -> p t k", k=HID),
                in_=xv[b, :, gg * TILES : (gg + 1) * TILES, :],
            )
            x_tiles[i] = x_sb

        def transpose_group(i):
            words = x_tiles[i][:].bitcast(F32)
            banks = []
            for pr in range(2):
                xt = ps_x.tile([P, 512], F32, name="xt", tag="xt")
                for j in range(2):
                    for u in range(2):
                        col = (2 * pr + j) * 256 + u * P
                        nc.tensor.transpose(
                            xt[:, u * 256 + j * P : u * 256 + (j + 1) * P],
                            words[:, col : col + P],
                            ident[:],
                        )
                banks.append(xt)
            xt_tiles[i] = banks

        def copy_group(i):
            grouped = gpool.tile([P, TILES * HID], BF16, name="grouped", tag="grouped", align_bytes=64)
            gw = grouped[:].bitcast(F32)
            for pr in range(2):
                nc.scalar.copy(
                    out=gw[:, pr * 512 : (pr + 1) * 512].rearrange("p (m u) -> p m u", u=2),
                    in_=xt_tiles[i][pr][:].rearrange("p (u m) -> p m u", u=2),
                )
            grouped_tiles[i] = grouped

        def quantise_group(i):
            codes = cpool.tile([P, TILES * P], U32, name="codes", tag="codes", align_bytes=64)
            scales = cpool.tile([P, TILES * P], U8, name="scales", tag="scales", align_bytes=64)
            nc.vector.quantize_mx(
                out=codes[:].bitcast(FP8X4), scales=scales[:], in_=grouped_tiles[i][:]
            )
            code_tiles[i] = (codes, scales)

        def project_group(i):
            codes, scales = code_tiles[i]
            v_ps = ps_v.tile([P, 512], F32, name="v_ps", tag="v_ps")
            banks = []
            for pr in range(2):
                qk_ps = ps_qk.tile([P, 512], F32, name="qk_ps", tag="qk_ps")
                for j in range(2):
                    tl = 2 * pr + j
                    cols = slice(tl * P, (tl + 1) * P)
                    nc.tensor.matmul_mx(
                        out=qk_ps[:, j * QK_COLS : (j + 1) * QK_COLS],
                        lhsT=codes[:, cols].bitcast(FP8X4),
                        lhsT_scale=scales[:, cols],
                        rhs=w_codes[:, 0:QK_COLS].bitcast(FP8X4),
                        rhs_scale=w_scales[:, 0:QK_COLS],
                        start=True,
                        stop=True,
                    )
                    nc.tensor.matmul_mx(
                        out=v_ps[:, cols],
                        lhsT=codes[:, cols].bitcast(FP8X4),
                        lhsT_scale=scales[:, cols],
                        rhs=w_codes[:, QK_COLS : QK_COLS + V_COLS].bitcast(FP8X4),
                        rhs_scale=w_scales[:, QK_COLS : QK_COLS + V_COLS],
                        start=True,
                        stop=True,
                    )
                banks.append(qk_ps)
            qk_banks[i] = banks
            v_banks[i] = v_ps

        def rope_products(i, pr):
            gg = i % GROUPS_PER_BATCH
            if pr == 0:
                pa = rpool.tile([P, TILES * QK_COLS], F32, name="pa", tag="pa")
                pb = rpool.tile([P, TILES * QK_COLS], F32, name="pb", tag="pb")
                prod_tiles[i] = (pa, pb)
            pa, pb = prod_tiles[i]
            t0 = gg * TILES + 2 * pr
            bank = qk_banks[i][pr][:].rearrange("p (j h d) -> p j h d", j=2, d=HEAD)
            pa_v = pa[:].rearrange("p (t h d) -> p t h d", t=TILES, d=HEAD)[:, 2 * pr : 2 * pr + 2, :, :]
            pb_v = pb[:].rearrange("p (t h d) -> p t h d", t=TILES, d=HEAD)[:, 2 * pr : 2 * pr + 2, :, :]
            nc.vector.tensor_tensor(
                out=pa_v,
                in0=bank,
                in1=cos_v[:, t0 : t0 + 2, :].unsqueeze(2).to_broadcast([P, 2, 4, HEAD]),
                op=MULT,
            )
            nc.vector.tensor_tensor(
                out=pb_v[:, :, :, 0:HALF],
                in0=bank[:, :, :, HALF:HEAD],
                in1=sin_v[:, t0 : t0 + 2, 0:HALF].unsqueeze(2).to_broadcast([P, 2, 4, HALF]),
                op=MULT,
            )
            nc.vector.tensor_tensor(
                out=pb_v[:, :, :, HALF:HEAD],
                in0=bank[:, :, :, 0:HALF],
                in1=sin_v[:, t0 : t0 + 2, HALF:HEAD].unsqueeze(2).to_broadcast([P, 2, 4, HALF]),
                op=MULT,
            )

        def rope_sum(i, engine, t_lo, t_hi):
            pa, pb = prod_tiles[i]
            if i not in out_tiles:
                qk_out = opool.tile([P, 2 * TILES * P], F32, name="qk_out", tag="qk_out")
                out_tiles[i] = qk_out
            qk_out = out_tiles[i]
            engine.tensor_tensor(
                out=qk_out[:].rearrange("p (g t c) -> p t g c", g=2, c=P)[:, t_lo:t_hi, :, :],
                in0=pa[:].rearrange("p (t g c) -> p t g c", g=2, c=P)[:, t_lo:t_hi, :, :],
                in1=pb[:].rearrange("p (t g c) -> p t g c", g=2, c=P)[:, t_lo:t_hi, :, :],
                op=ADD,
            )

        def copy_v(i):
            v_out = opool.tile([P, TILES * P], F32, name="v_out", tag="v_out")
            nc.scalar.copy(out=v_out[:], in_=v_banks[i][:])
            return v_out

        def store_v(i, v_out):
            b, gg = divmod(i, GROUPS_PER_BATCH)
            ts = slice(gg * TILES, (gg + 1) * TILES)
            nc.sync.dma_start(out=vv[b, :, ts, :], in_=v_out[:].rearrange("p (t c) -> p t c", c=P))

        def store_qk(i, t_lo, t_hi):
            b, gg = divmod(i, GROUPS_PER_BATCH)
            ts = slice(gg * TILES + t_lo, gg * TILES + t_hi)
            qk_v = out_tiles[i][:].rearrange("p (g t c) -> p g t c", g=2, c=P)
            nc.sync.dma_start(out=qv[b, :, ts, :], in_=qk_v[:, 0, t_lo:t_hi, :])
            nc.sync.dma_start(out=kv[b, :, ts, :], in_=qk_v[:, 1, t_lo:t_hi, :])

        load_x(0)
        nc.sync.dma_start(
            out=w_raw[:].rearrange("q (u f) -> q u f", u=2),
            in_=w_qkv.rearrange("(u q e) c -> q u (e c)", u=2, e=2),
        )
        load_x(1)
        nc.sync.dma_start(out=cos_v, in_=cos.rearrange("(p t) d -> p t d", t=T_PER_PART))
        nc.sync.dma_start(out=sin_v, in_=sin.rearrange("(p t) d -> p t d", t=T_PER_PART))
        for i in range(2, N_GROUPS):
            load_x(i)

        nc.vector.tensor_copy(
            out=w_grp[:].rearrange("p (c t) -> p c t", t=4),
            in_=w_raw[:].rearrange("p (t c) -> p c t", t=4),
        )
        nc.vector.quantize_mx(
            out=w_codes[:, 0:QK_COLS].bitcast(FP8X4),
            scales=w_scales[:, 0:QK_COLS],
            in_=w_grp[:, 0 : 4 * QK_COLS],
        )
        nc.vector.quantize_mx(
            out=w_codes[:, QK_COLS : QK_COLS + V_COLS].bitcast(FP8X4),
            scales=w_scales[:, QK_COLS : QK_COLS + V_COLS],
            in_=w_grp[:, 4 * QK_COLS : 4 * (QK_COLS + V_COLS)],
        )

        transpose_group(0)
        copy_group(0)
        quantise_group(0)
        transpose_group(1)
        copy_group(1)
        quantise_group(1)
        nc.vector.tensor_scalar_mul(out=sin_v[:, :, 0:HALF], in0=sin_v[:, :, 0:HALF], scalar1=-1.0)
        project_group(0)

        for i in range(N_GROUPS):
            if i + 2 < N_GROUPS:
                transpose_group(i + 2)
            v_out = copy_v(i)
            if i + 2 < N_GROUPS:
                copy_group(i + 2)
            if i + 1 < N_GROUPS:
                project_group(i + 1)
            if i + 1 < N_GROUPS:
                rope_products(i, 0)
                rope_products(i, 1)
                if i + 2 < N_GROUPS:
                    quantise_group(i + 2)
                rope_sum(i, nc.gpsimd, 0, TILES)
                store_v(i, v_out)
                store_qk(i, 0, TILES)
            else:
                store_v(i, v_out)
                for pr in range(2):
                    rope_products(i, pr)
                    rope_sum(i, nc.vector, 2 * pr, 2 * pr + 2)
                    store_qk(i, 2 * pr, 2 * pr + 2)
